import numpy as np
import ml_dtypes


def mxq(x, axis, fmt="e4m3"):
    dtype, down = {"e4m3": (ml_dtypes.float8_e4m3fn, 7), "e5m2": (ml_dtypes.float8_e5m2, 14)}[fmt]
    v = np.moveaxis(np.asarray(x, np.float32).astype(ml_dtypes.bfloat16).astype(np.float64), axis, -1)
    blocks = v.reshape(v.shape[:-1] + (-1, 32))
    amax = np.abs(blocks).max(-1, keepdims=True)
    byte = np.maximum(np.where(amax > 0, np.frexp(amax)[1] - 1 + 127, 0) - down, 1)
    scale = np.exp2(byte - 127.0)
    codes = (blocks / scale).astype(np.float32).astype(dtype).astype(np.float64)
    return np.moveaxis((codes * scale).reshape(v.shape), -1, axis)


WIDE = False


def mx_kscale(k):
    if not WIDE:
        return np.ones(k)
    levels = np.array([10, -10, 5, -5, 0])
    if k % 512:
        return np.exp2(np.random.permutation(np.resize(levels, k // 32))).repeat(32)
    a = np.empty((k // 512, 16))
    for p in range(k // 512):
        a[p, :8] = np.random.permutation(np.resize(levels, 8))
        for g in range(8):
            far = levels[np.abs(levels - a[p, g]) >= 10]
            a[p, g + 8] = far[np.random.randint(len(far))]
    return np.exp2(a.ravel()).repeat(32)


BF16 = ml_dtypes.bfloat16


def bf(x):
    return np.asarray(x, np.float32).astype(BF16)


def f64(x):
    return np.asarray(x).astype(np.float64)


E2M1 = np.array([0.0, 0.5, 1.0, 1.5, 2.0, 3.0, 4.0, 6.0, -0.0, -0.5, -1.0, -1.5, -2.0, -3.0, -4.0, -6.0])


def pack_weight(w, fmt):
    k, n = w.shape
    w = f64(bf(w)).reshape(k // 32, 32, n)
    amax = np.abs(w).max(1)
    if fmt == "e4m3":
        byte = np.frexp(amax)[1] - 1 + 127 - 7
    else:
        mant, ex = np.frexp(amax / 6.0)
        byte = np.where(mant > 0.5, ex, ex - 1) + 127
    byte = np.clip(np.where(amax > 0, byte, 1), 1, 254)
    scaled = (w * np.exp2(127.0 - byte)[:, None, :]).reshape(k, n).astype(np.float32)
    by_word = np.ascontiguousarray(scaled.reshape(k // 512, 128, 4, n).transpose(0, 1, 3, 2))
    if fmt == "e4m3":
        words = by_word.astype(ml_dtypes.float8_e4m3fn).view(np.uint8)
    else:
        c = by_word.astype(ml_dtypes.float4_e2m1fn).view(np.uint8) & 0xF
        words = c[..., 0::2] | (c[..., 1::2] << 4)
    return np.ascontiguousarray(words), np.ascontiguousarray(byte.astype(np.uint8).reshape(k // 512, 16, n))


def unpack_weight(words, scales, fmt):
    g, p, n, _ = words.shape
    if fmt == "e4m3":
        vals = np.ascontiguousarray(words).view(ml_dtypes.float8_e4m3fn).astype(np.float64)
    else:
        nib = np.empty((g, p, n, 4), np.uint8)
        nib[..., 0::2] = words & 0xF
        nib[..., 1::2] = words >> 4
        vals = E2M1[nib]
    vals = vals * np.repeat(np.exp2(scales.astype(np.float64) - 127.0), 8, axis=1)[..., None]
    return vals.transpose(0, 1, 3, 2).reshape(g * 512, n)

def pack4(w):
    words, scales = pack_weight(w, "e2m1")
    return words.reshape(words.shape[0], 128, -1), scales


def unpack4(words, scales):
    return unpack_weight(words.reshape(words.shape[0], 128, -1, 2), scales, "e2m1")


B, I, H = 512, 1024, 1024
G = 4
MXH = H % 512 == 0


def sigmoid(v):
    return 1.0 / (1.0 + np.exp(-v))


def setup_inputs():
    s = mx_kscale(I)
    t = mx_kscale(H) if MXH else np.ones(H)
    x = bf(np.random.standard_normal((B, I)) * s)
    h = bf(np.random.standard_normal((B, H)) * t)
    c = bf(np.random.standard_normal((B, H)))
    wx = np.random.standard_normal((G, H, I)) * 0.8 / np.sqrt(I) / s
    cat = np.ascontiguousarray(wx.swapaxes(1, 2)).reshape(-1, H)
    Wx_words, Wx_scales = pack4(cat)
    Wh = bf(np.random.standard_normal((4, H, H)) * 0.8 / np.sqrt(H) / t)
    bx = bf(np.random.standard_normal((4, H)) * 0.3)
    bh = bf(np.random.standard_normal((4, H)) * 0.3)
    return {"x": x, "h": h, "c": c, "Wx_words": Wx_words, "Wx_scales": Wx_scales,
            "Wh": Wh, "bx": bx, "bh": bh}


def reference(x, h, c, Wx_words, Wx_scales, Wh, bx, bh):
    wx = unpack4(Wx_words, Wx_scales).reshape(G, I, H).swapaxes(1, 2).reshape(G * H, I)
    wh = f64(Wh).reshape(4 * H, H)
    gx = (mxq(f64(x), 1, "e4m3") @ wx.T) + f64(bx).reshape(-1)
    if MXH:
        gh = (mxq(f64(h), 1, "e4m3") @ mxq(wh, 1, "e4m3").T) + f64(bh).reshape(-1)
    else:
        gh = f64(h) @ wh.T + f64(bh).reshape(-1)
    g = (gx + gh).reshape(-1, 4, H)
    i = sigmoid(g[:, 0])
    f = sigmoid(g[:, 1])
    gc = np.tanh(g[:, 2])
    o = sigmoid(g[:, 3])
    c_new = f * f64(c) + i * gc
    hs = o * np.tanh(c_new)
    return (hs, c_new)

@@ -1,0 +1,216 @@
+from contextlib import ExitStack
+
+import concourse.mybir as mybir
+from concourse.masks import make_identity
+
+F32 = mybir.dt.float32
+BF16 = mybir.dt.bfloat16
+I32 = mybir.dt.int32
+U32 = mybir.dt.uint32
+U8 = mybir.dt.uint8
+FP8X4 = mybir.dt.float8_e4m3fn_x4
+FP4X4 = mybir.dt.float4_e2m1fn_x4
+SIGMOID = mybir.ActivationFunctionType.Sigmoid
+TANH = mybir.ActivationFunctionType.Tanh
+
+P = 128
+PACK = 4
+K_PASS = P * PACK
+BATCH = 512
+K = 1024
+HIDDEN = 1024
+PASSES = K // K_PASS
+BLOCK_ROWS = 512
+ROW_TILES = BLOCK_ROWS // P
+WORDS = K // 2
+PASS_WORDS = K_PASS // 2
+HALVES = HIDDEN // BLOCK_ROWS
+
+GATE_I, GATE_F, GATE_G, GATE_O = 0, 1, 2, 3
+WH_SCALAR_TILES = 3
+TANH_LAG = 2
+
+FLOPS = 2 * BATCH * 4 * HIDDEN * 2 * K
+
+
+def tile_lstmcell_e_kernel(tc, x, h, c, Wx_words, Wx_scales, Wh, bx, bh, out_0, out_1):
+    nc = tc.nc
+    blocks = [(half, gate) for half in range(HALVES) for gate in (GATE_F, GATE_I, GATE_G)]
+    blocks += [(half, GATE_O) for half in range(HALVES)]
+
+    with ExitStack() as ctx:
+        keep = ctx.enter_context(tc.tile_pool(name="keep", bufs=1))
+        raw_pool = ctx.enter_context(tc.tile_pool(name="raw", bufs=len(blocks) + 2))
+        grouped_pool = ctx.enter_context(tc.tile_pool(name="grouped", bufs=2))
+        wh_mx_pool = ctx.enter_context(tc.tile_pool(name="wh_mx", bufs=2))
+        bias_pool = ctx.enter_context(tc.tile_pool(name="bias", bufs=2))
+        gate_pool = ctx.enter_context(tc.tile_pool(name="gates", bufs=HALVES * ROW_TILES))
+        flip_psum = ctx.enter_context(tc.psum_pool(name="flip", bufs=ROW_TILES))
+        sum_psum = ctx.enter_context(tc.psum_pool(name="sums", bufs=ROW_TILES))
+        ctx.enter_context(tc.manual_schedule())
+
+        wx_planes = keep.tile([P, 4 * PASSES, HIDDEN], U8, align_bytes=64)
+        nc.vector.memset(wx_planes[:].rearrange("p s n -> p (s n)").bitcast(I32), 0)
+        bias_rows = keep.tile([P, 4 * HIDDEN], BF16)
+        nc.vector.memset(bias_rows[:].bitcast(I32), 0)
+        ones = keep.tile([P, P], BF16)
+        nc.vector.memset(ones[:], 1.0)
+        warm = keep.tile([P, 1], F32)
+        nc.vector.memset(warm[:], 0.0)
+        identity = keep.tile([P, P], F32)
+        make_identity(nc, identity[:])
+        nc.scalar.activation(out=warm[:], in_=warm[:], func=SIGMOID)
+
+        def load_rows(rows):
+            raw = raw_pool.tile([P, ROW_TILES, K], BF16)
+            nc.sync.dma_start(out=raw[:], in_=rows.rearrange("(r p) k -> p r k", p=P))
+            return raw
+
+        x_raw = load_rows(x)
+        h_raw = load_rows(h)
+        nc.gpsimd.dma_start(out=bias_rows[0:1, :], in_=bx.rearrange("(o g) n -> o (g n)", o=1))
+        nc.gpsimd.dma_start(out=bias_rows[1:2, :], in_=bh.rearrange("(o g) n -> o (g n)", o=1))
+
+        wx_words = keep.tile([P, 4 * PASSES, 2 * HIDDEN], U8, align_bytes=64)
+        words_dram = Wx_words.bitcast(I32)
+        scales_dram = Wx_scales.bitcast(I32).rearrange("s (q r) n -> r q s n", r=4)
+        c_sb = keep.tile([P, ROW_TILES, HIDDEN], BF16)
+        wh_raw = []
+        for n in range(len(blocks)):
+            half, gate = blocks[n]
+            wh_raw.append(load_rows(Wh[gate, half * BLOCK_ROWS : (half + 1) * BLOCK_ROWS, :]))
+            if n == 0:
+                for r in range(4):
+                    nc.sync.dma_start(out=wx_planes[r:P:32, :, :].bitcast(I32), in_=scales_dram[r])
+            if half == 0:
+                first, last = gate * PASSES, (gate + 1) * PASSES
+                nc.sync.dma_start(
+                    out=wx_words[:, first:last, :].bitcast(I32),
+                    in_=words_dram[first:last].rearrange("s p n -> p s n"),
+                )
+            if n == 1:
+                nc.sync.dma_start(out=c_sb[:], in_=c.rearrange("(b p) n -> p b n", p=P))
+
+        def transpose_block(raw, k_step, scalar_tiles):
+            grouped = grouped_pool.tile([P, PASSES, BLOCK_ROWS, PACK], BF16, align_bytes=64)
+            for r in range(ROW_TILES):
+                words = raw[:, r, :].bitcast(F32)
+                flipped = flip_psum.tile([P, PASSES, 2, P], F32, tag="bank")
+                for s in range(PASSES):
+                    for u in range(2):
+                        if k_step == 2:
+                            cols = words[:, s * PASS_WORDS + u : (s + 1) * PASS_WORDS : 2]
+                        else:
+                            cols = words[:, s * PASS_WORDS + u * P : s * PASS_WORDS + (u + 1) * P]
+                        nc.tensor.transpose(flipped[:, s, u, :], cols, identity[:])
+                copy_out = nc.scalar.copy if r < scalar_tiles else nc.vector.tensor_copy
+                copy_out(
+                    out=grouped[:, :, r * P : (r + 1) * P, :].bitcast(F32),
+                    in_=flipped[:].rearrange("p s u n -> p s n u"),
+                )
+            return grouped
+
+        def quantise(grouped, codes, planes):
+            nc.vector.quantize_mx(
+                out=codes[:].rearrange("p s n -> p (s n)").bitcast(FP8X4),
+                scales=planes[:].rearrange("p s n -> p (s n)"),
+                in_=grouped[:].rearrange("p s n t -> p (s n t)"),
+            )
+
+        x_codes = keep.tile([P, PASSES, BATCH], U32, align_bytes=64)
+        x_planes = keep.tile([P, PASSES, BATCH], U8, align_bytes=64)
+        h_codes = keep.tile([P, PASSES, BATCH], U32, align_bytes=64)
+        h_planes = keep.tile([P, PASSES, BATCH], U8, align_bytes=64)
+        x_grouped = transpose_block(x_raw, 2, 0)
+        h_grouped = transpose_block(h_raw, 2, 0)
+        quantise(x_grouped, x_codes, x_planes)
+        quantise(h_grouped, h_codes, h_planes)
+
+        wh_grouped = {}
+        wh_mx = {}
+        bias = {}
+        gates = {}
+
+        def prepare(n):
+            half, gate = blocks[n]
+            wh_grouped[n] = transpose_block(wh_raw[n], 2, WH_SCALAR_TILES)
+            start_col = gate * HIDDEN + half * BLOCK_ROWS
+            spread = flip_psum.tile([P, BLOCK_ROWS], F32, tag="bank")
+            nc.tensor.matmul(
+                spread[:], lhsT=ones[:], rhs=bias_rows[:, start_col : start_col + BLOCK_ROWS], start=True, stop=True
+            )
+            bias[n] = bias_pool.tile([P, BLOCK_ROWS], F32, name="bias_sb")
+            nc.vector.tensor_copy(out=bias[n][:], in_=spread[:])
+
+        def quantise_block(n):
+            codes = wh_mx_pool.tile([P, PASSES, BLOCK_ROWS], U32, name="wh_codes", align_bytes=64)
+            planes = wh_mx_pool.tile([P, PASSES, BLOCK_ROWS], U8, name="wh_planes", align_bytes=64)
+            quantise(wh_grouped[n], codes, planes)
+            wh_mx[n] = (codes, planes)
+
+        def x_passes(n):
+            half, gate = blocks[n]
+            for b in range(ROW_TILES):
+                sums[b] = sum_psum.tile([P, BLOCK_ROWS], F32, name="acc")
+                for s in range(PASSES):
+                    nc.tensor.matmul_mx(
+                        out=sums[b][:],
+                        lhsT=x_codes[:, s, b * P : (b + 1) * P].bitcast(FP8X4),
+                        lhsT_scale=x_planes[:, s, b * P : (b + 1) * P],
+                        rhs=wx_words[
+                            :, gate * PASSES + s, 2 * half * BLOCK_ROWS : 2 * (half + 1) * BLOCK_ROWS
+                        ].bitcast(FP4X4),
+                        rhs_scale=wx_planes[:, gate * PASSES + s, half * BLOCK_ROWS : (half + 1) * BLOCK_ROWS],
+                        start=(s == 0),
+                        stop=False,
+                    )
+
+        def h_passes(n, b):
+            half, gate = blocks[n]
+            wh_codes, wh_planes = wh_mx[n]
+            for s in range(PASSES):
+                nc.tensor.matmul_mx(
+                    out=sums[b][:],
+                    lhsT=h_codes[:, s, b * P : (b + 1) * P].bitcast(FP8X4),
+                    lhsT_scale=h_planes[:, s, b * P : (b + 1) * P],
+                    rhs=wh_codes[:, s, :].bitcast(FP8X4),
+                    rhs_scale=wh_planes[:, s, :],
+                    start=False,
+                    stop=(s == PASSES - 1),
+                )
+            value = gate_pool.tile([P, BLOCK_ROWS], F32, name="gate%d" % gate, tag="gate%d" % gate)
+            nc.vector.tensor_add(out=value[:], in0=sums[b][:], in1=bias[n][:])
+            nc.scalar.activation(out=value[:], in_=value[:], func=(TANH if gate == GATE_G else SIGMOID))
+            gates[(gate, half, b)] = value
+
+        sums = {}
+        prepare(0)
+        quantise_block(0)
+        for n in range(len(blocks)):
+            half, gate = blocks[n]
+            cols = slice(half * BLOCK_ROWS, (half + 1) * BLOCK_ROWS)
+            x_passes(n)
+            if n + 1 < len(blocks):
+                prepare(n + 1)
+            if n >= TANH_LAG and blocks[n - TANH_LAG][1] == GATE_G:
+                for b in range(ROW_TILES):
+                    earlier = blocks[n - TANH_LAG][0]
+                    nc.scalar.activation(
+                        out=gates[(GATE_G, earlier, b)][:], in_=gates[(GATE_F, earlier, b)][:], func=TANH
+                    )
+            for b in range(ROW_TILES):
+                h_passes(n, b)
+                f, i, g = [gates.get((e, half, b)) for e in (GATE_F, GATE_I, GATE_G)]
+                if gate == GATE_F:
+                    nc.gpsimd.tensor_mul(out=f[:], in0=f[:], in1=c_sb[:, b, cols])
+                if gate == GATE_G:
+                    nc.gpsimd.tensor_mul(out=i[:], in0=i[:], in1=g[:])
+                    nc.gpsimd.tensor_add(out=f[:], in0=f[:], in1=i[:])
+                    nc.sync.dma_start(out=out_1[b * P : (b + 1) * P, cols], in_=f[:])
+            if n + 1 < len(blocks):
+                quantise_block(n + 1)
+            if gate == GATE_O:
+                for b in range(ROW_TILES):
+                    hs = gates[(GATE_O, half, b)]
+                    nc.vector.tensor_mul(out=hs[:], in0=hs[:], in1=gates[(GATE_G, half, b)][:])
+                    nc.sync.dma_start(out=out_0[b * P : (b + 1) * P, cols], in_=hs[:])

@@ -22,9 +22,9 @@ HIDDEN = 1024
 PASSES = K // K_PASS
 BLOCK_ROWS = 512
 ROW_TILES = BLOCK_ROWS // P
-WORDS = K // 2
 PASS_WORDS = K_PASS // 2
 HALVES = HIDDEN // BLOCK_ROWS
+CHUNKS = 4 * HALVES
 
 GATE_I, GATE_F, GATE_G, GATE_O = 0, 1, 2, 3
 WH_SCALAR_TILES = 3
@@ -43,124 +43,167 @@ def tile_lstmcell_e_kernel(tc, x, h, c, Wx_words, Wx_scales, Wh, bx, bh, out_0, 
         raw_pool = ctx.enter_context(tc.tile_pool(name="raw", bufs=len(blocks) + 2))
         grouped_pool = ctx.enter_context(tc.tile_pool(name="grouped", bufs=2))
         wh_mx_pool = ctx.enter_context(tc.tile_pool(name="wh_mx", bufs=2))
-        bias_pool = ctx.enter_context(tc.tile_pool(name="bias", bufs=2))
         gate_pool = ctx.enter_context(tc.tile_pool(name="gates", bufs=HALVES * ROW_TILES))
         flip_psum = ctx.enter_context(tc.psum_pool(name="flip", bufs=ROW_TILES))
         sum_psum = ctx.enter_context(tc.psum_pool(name="sums", bufs=ROW_TILES))
         ctx.enter_context(tc.manual_schedule())
 
-        wx_planes = keep.tile([P, 4 * PASSES, HIDDEN], U8, align_bytes=64)
-        nc.vector.memset(wx_planes[:].rearrange("p s n -> p (s n)").bitcast(I32), 0)
-        bias_rows = keep.tile([P, 4 * HIDDEN], BF16)
+        bias_rows = keep.tile([P, BLOCK_ROWS], BF16)
         nc.vector.memset(bias_rows[:].bitcast(I32), 0)
-        ones = keep.tile([P, P], BF16)
-        nc.vector.memset(ones[:], 1.0)
         warm = keep.tile([P, 1], F32)
         nc.vector.memset(warm[:], 0.0)
+        wx_planes = {}
+        for gate in (GATE_F, GATE_I, GATE_G, GATE_O):
+            wx_planes[gate] = keep.tile([P, PASSES, HIDDEN], U8, name="wx_planes%d" % gate, align_bytes=64)
+            nc.vector.memset(wx_planes[gate][:].rearrange("p s n -> p (s n)").bitcast(I32), 0)
         identity = keep.tile([P, P], F32)
         make_identity(nc, identity[:])
+        pick = keep.tile([P, CHUNKS], BF16)
+        nc.gpsimd.tensor_add(out=pick[:], in0=identity[:, 0:CHUNKS], in1=identity[:, CHUNKS : 2 * CHUNKS])
+
+        nc.scalar.dma_start(out=bias_rows[0:CHUNKS, :], in_=bx.rearrange("g (a n) -> (g a) n", n=BLOCK_ROWS))
+        nc.scalar.dma_start(
+            out=bias_rows[CHUNKS : 2 * CHUNKS, :], in_=bh.rearrange("g (a n) -> (g a) n", n=BLOCK_ROWS)
+        )
         nc.scalar.activation(out=warm[:], in_=warm[:], func=SIGMOID)
 
-        def load_rows(rows):
+        def load_rows(rows, pieces):
             raw = raw_pool.tile([P, ROW_TILES, K], BF16)
-            nc.sync.dma_start(out=raw[:], in_=rows.rearrange("(r p) k -> p r k", p=P))
+            step = ROW_TILES // pieces
+            for a in range(0, ROW_TILES, step):
+                nc.sync.dma_start(
+                    out=raw[:, a : a + step, :],
+                    in_=rows[a * P : (a + step) * P, :].rearrange("(r p) k -> p r k", p=P),
+                )
             return raw
 
-        x_raw = load_rows(x)
-        h_raw = load_rows(h)
-        nc.gpsimd.dma_start(out=bias_rows[0:1, :], in_=bx.rearrange("(o g) n -> o (g n)", o=1))
-        nc.gpsimd.dma_start(out=bias_rows[1:2, :], in_=bh.rearrange("(o g) n -> o (g n)", o=1))
-
-        wx_words = keep.tile([P, 4 * PASSES, 2 * HIDDEN], U8, align_bytes=64)
+        wx_words = {}
         words_dram = Wx_words.bitcast(I32)
         scales_dram = Wx_scales.bitcast(I32).rearrange("s (q r) n -> r q s n", r=4)
-        c_sb = keep.tile([P, ROW_TILES, HIDDEN], BF16)
-        wh_raw = []
-        for n in range(len(blocks)):
-            half, gate = blocks[n]
-            wh_raw.append(load_rows(Wh[gate, half * BLOCK_ROWS : (half + 1) * BLOCK_ROWS, :]))
-            if n == 0:
-                for r in range(4):
-                    nc.sync.dma_start(out=wx_planes[r:P:32, :, :].bitcast(I32), in_=scales_dram[r])
-            if half == 0:
-                first, last = gate * PASSES, (gate + 1) * PASSES
-                nc.sync.dma_start(
-                    out=wx_words[:, first:last, :].bitcast(I32),
-                    in_=words_dram[first:last].rearrange("s p n -> p s n"),
-                )
-            if n == 1:
-                nc.sync.dma_start(out=c_sb[:], in_=c.rearrange("(b p) n -> p b n", p=P))
 
-        def transpose_block(raw, k_step, scalar_tiles):
-            grouped = grouped_pool.tile([P, PASSES, BLOCK_ROWS, PACK], BF16, align_bytes=64)
-            for r in range(ROW_TILES):
-                words = raw[:, r, :].bitcast(F32)
-                flipped = flip_psum.tile([P, PASSES, 2, P], F32, tag="bank")
-                for s in range(PASSES):
-                    for u in range(2):
-                        if k_step == 2:
-                            cols = words[:, s * PASS_WORDS + u : (s + 1) * PASS_WORDS : 2]
-                        else:
-                            cols = words[:, s * PASS_WORDS + u * P : s * PASS_WORDS + (u + 1) * P]
-                        nc.tensor.transpose(flipped[:, s, u, :], cols, identity[:])
-                copy_out = nc.scalar.copy if r < scalar_tiles else nc.vector.tensor_copy
-                copy_out(
-                    out=grouped[:, :, r * P : (r + 1) * P, :].bitcast(F32),
-                    in_=flipped[:].rearrange("p s u n -> p s n u"),
+        def load_scales(gate):
+            for r in range(4):
+                nc.sync.dma_start(
+                    out=wx_planes[gate][r:P:32, :, :].bitcast(I32),
+                    in_=scales_dram[r, :, gate * PASSES : (gate + 1) * PASSES, :],
                 )
-            return grouped
+
+        def load_words(gate, half):
+            words = keep.tile(
+                [P, PASSES, 2 * BLOCK_ROWS], U8, name="wx_words%d_%d" % (gate, half), align_bytes=64
+            )
+            first = half * BLOCK_ROWS // 2
+            nc.sync.dma_start(
+                out=words[:].bitcast(I32),
+                in_=words_dram[gate * PASSES : (gate + 1) * PASSES, :, first : first + BLOCK_ROWS // 2].rearrange(
+                    "s p n -> p s n"
+                ),
+            )
+            wx_words[(gate, half)] = words
+
+        def load_wh(n):
+            half, gate = blocks[n]
+            return load_rows(Wh[gate, half * BLOCK_ROWS : (half + 1) * BLOCK_ROWS, :], 1)
+
+        c_sb = keep.tile([P, ROW_TILES, HIDDEN], BF16)
+        wh_raw = {}
+        x_raw = load_rows(x, 4)
+        load_scales(GATE_F)
+        load_words(GATE_F, 0)
+        h_raw = load_rows(h, 2)
+        wh_raw[0] = load_wh(0)
+        wh_raw[1] = load_wh(1)
+        for gate in (GATE_I, GATE_G, GATE_O):
+            load_scales(gate)
+        load_words(GATE_I, 0)
+        wh_raw[2] = load_wh(2)
+        load_words(GATE_G, 0)
+        nc.sync.dma_start(out=c_sb[:], in_=c.rearrange("(b p) n -> p b n", p=P))
+        for n in range(3, len(blocks)):
+            half, gate = blocks[n]
+            load_words(gate, half)
+            wh_raw[n] = load_wh(n)
+
+        bias_sb = keep.tile([P, CHUNKS, BLOCK_ROWS], F32)
+
+        def spread_bias(q):
+            spread = sum_psum.tile([P, BLOCK_ROWS], F32, name="spread", tag="sum")
+            nc.tensor.matmul(
+                spread[:], lhsT=pick[:, q : q + 1].to_broadcast([P, P]), rhs=bias_rows[:], start=True, stop=True
+            )
+            nc.scalar.copy(out=bias_sb[:, q, :], in_=spread[:])
+
+        def transpose_tile(raw, r, out, copy_out):
+            words = raw[:, r, :].bitcast(F32)
+            flipped = flip_psum.tile([P, PASSES, 2, P], F32, tag="bank")
+            for s in range(PASSES):
+                for u in range(2):
+                    nc.tensor.transpose(
+                        flipped[:, s, u, :], words[:, s * PASS_WORDS + u : (s + 1) * PASS_WORDS : 2], identity[:]
+                    )
+            copy_out(out=out.bitcast(F32), in_=flipped[:].rearrange("p s u n -> p s n u"))
 
         def quantise(grouped, codes, planes):
-            nc.vector.quantize_mx(
-                out=codes[:].rearrange("p s n -> p (s n)").bitcast(FP8X4),
-                scales=planes[:].rearrange("p s n -> p (s n)"),
-                in_=grouped[:].rearrange("p s n t -> p (s n t)"),
+            nc.vector.quantize_mx(out=codes.bitcast(FP8X4), scales=planes, in_=grouped)
+
+        def operand(name):
+            codes = keep.tile([P, ROW_TILES, PASSES, P], U32, name=name + "_codes", align_bytes=64)
+            planes = keep.tile([P, ROW_TILES, PASSES, P], U8, name=name + "_planes", align_bytes=64)
+            return codes, planes
+
+        def quantise_tile(grouped, mx, r):
+            quantise(
+                grouped[:, r, :, :, :].rearrange("p s n t -> p (s n t)"),
+                mx[0][:, r, :, :].rearrange("p s n -> p (s n)"),
+                mx[1][:, r, :, :].rearrange("p s n -> p (s n)"),
             )
 
-        x_codes = keep.tile([P, PASSES, BATCH], U32, align_bytes=64)
-        x_planes = keep.tile([P, PASSES, BATCH], U8, align_bytes=64)
-        h_codes = keep.tile([P, PASSES, BATCH], U32, align_bytes=64)
-        h_planes = keep.tile([P, PASSES, BATCH], U8, align_bytes=64)
-        x_grouped = transpose_block(x_raw, 2, 0)
-        h_grouped = transpose_block(h_raw, 2, 0)
-        quantise(x_grouped, x_codes, x_planes)
-        quantise(h_grouped, h_codes, h_planes)
+        def stationary(raw, mx, scalar_tiles):
+            grouped = grouped_pool.tile([P, ROW_TILES, PASSES, P, PACK], BF16, name="kept_grouped", tag="grouped", align_bytes=64)
+            for r in range(ROW_TILES):
+                transpose_tile(
+                    raw, r, grouped[:, r, :, :, :], nc.scalar.copy if r in scalar_tiles else nc.vector.tensor_copy
+                )
+                if r > 0:
+                    quantise_tile(grouped, mx, r - 1)
+            quantise_tile(grouped, mx, ROW_TILES - 1)
 
         wh_grouped = {}
         wh_mx = {}
-        bias = {}
         gates = {}
+        sums = {}
 
-        def prepare(n):
-            half, gate = blocks[n]
-            wh_grouped[n] = transpose_block(wh_raw[n], 2, WH_SCALAR_TILES)
-            start_col = gate * HIDDEN + half * BLOCK_ROWS
-            spread = flip_psum.tile([P, BLOCK_ROWS], F32, tag="bank")
-            nc.tensor.matmul(
-                spread[:], lhsT=ones[:], rhs=bias_rows[:, start_col : start_col + BLOCK_ROWS], start=True, stop=True
-            )
-            bias[n] = bias_pool.tile([P, BLOCK_ROWS], F32, name="bias_sb")
-            nc.vector.tensor_copy(out=bias[n][:], in_=spread[:])
+        def transpose_block(n, scalar_tiles):
+            wh_grouped[n] = grouped_pool.tile([P, PASSES, BLOCK_ROWS, PACK], BF16, name="wh_grouped", tag="grouped", align_bytes=64)
+            for r in range(ROW_TILES):
+                transpose_tile(
+                    wh_raw[n],
+                    r,
+                    wh_grouped[n][:, :, r * P : (r + 1) * P, :],
+                    nc.scalar.copy if r in scalar_tiles else nc.vector.tensor_copy,
+                )
 
         def quantise_block(n):
             codes = wh_mx_pool.tile([P, PASSES, BLOCK_ROWS], U32, name="wh_codes", align_bytes=64)
             planes = wh_mx_pool.tile([P, PASSES, BLOCK_ROWS], U8, name="wh_planes", align_bytes=64)
-            quantise(wh_grouped[n], codes, planes)
+            quantise(
+                wh_grouped[n][:].rearrange("p s n t -> p (s n t)"),
+                codes[:].rearrange("p s n -> p (s n)"),
+                planes[:].rearrange("p s n -> p (s n)"),
+            )
             wh_mx[n] = (codes, planes)
 
         def x_passes(n):
             half, gate = blocks[n]
             for b in range(ROW_TILES):
-                sums[b] = sum_psum.tile([P, BLOCK_ROWS], F32, name="acc")
+                sums[b] = sum_psum.tile([P, BLOCK_ROWS], F32, name="acc", tag="sum")
                 for s in range(PASSES):
                     nc.tensor.matmul_mx(
                         out=sums[b][:],
-                        lhsT=x_codes[:, s, b * P : (b + 1) * P].bitcast(FP8X4),
-                        lhsT_scale=x_planes[:, s, b * P : (b + 1) * P],
-                        rhs=wx_words[
-                            :, gate * PASSES + s, 2 * half * BLOCK_ROWS : 2 * (half + 1) * BLOCK_ROWS
-                        ].bitcast(FP4X4),
-                        rhs_scale=wx_planes[:, gate * PASSES + s, half * BLOCK_ROWS : (half + 1) * BLOCK_ROWS],
+                        lhsT=x_mx[0][:, b, s, :].bitcast(FP8X4),
+                        lhsT_scale=x_mx[1][:, b, s, :],
+                        rhs=wx_words[(gate, half)][:, s, :].bitcast(FP4X4),
+                        rhs_scale=wx_planes[gate][:, s, half * BLOCK_ROWS : (half + 1) * BLOCK_ROWS],
                         start=(s == 0),
                         stop=False,
                     )
@@ -171,27 +214,35 @@ def tile_lstmcell_e_kernel(tc, x, h, c, Wx_words, Wx_scales, Wh, bx, bh, out_0, 
             for s in range(PASSES):
                 nc.tensor.matmul_mx(
                     out=sums[b][:],
-                    lhsT=h_codes[:, s, b * P : (b + 1) * P].bitcast(FP8X4),
-                    lhsT_scale=h_planes[:, s, b * P : (b + 1) * P],
+                    lhsT=h_mx[0][:, b, s, :].bitcast(FP8X4),
+                    lhsT_scale=h_mx[1][:, b, s, :],
                     rhs=wh_codes[:, s, :].bitcast(FP8X4),
                     rhs_scale=wh_planes[:, s, :],
                     start=False,
                     stop=(s == PASSES - 1),
                 )
             value = gate_pool.tile([P, BLOCK_ROWS], F32, name="gate%d" % gate, tag="gate%d" % gate)
-            nc.vector.tensor_add(out=value[:], in0=sums[b][:], in1=bias[n][:])
+            nc.vector.tensor_add(out=value[:], in0=sums[b][:], in1=bias_sb[:, gate * HALVES + half, :])
             nc.scalar.activation(out=value[:], in_=value[:], func=(TANH if gate == GATE_G else SIGMOID))
             gates[(gate, half, b)] = value
 
-        sums = {}
-        prepare(0)
+        x_mx = operand("x")
+        h_mx = operand("h")
+        stationary(x_raw, x_mx, ())
+        for q in range(CHUNKS):
+            spread_bias(q)
+        x_passes(0)
+        stationary(h_raw, h_mx, (0, 2))
+        transpose_block(0, (0, 2))
         quantise_block(0)
+
         for n in range(len(blocks)):
             half, gate = blocks[n]
             cols = slice(half * BLOCK_ROWS, (half + 1) * BLOCK_ROWS)
-            x_passes(n)
+            if n > 0:
+                x_passes(n)
             if n + 1 < len(blocks):
-                prepare(n + 1)
+                transpose_block(n + 1, range(WH_SCALAR_TILES))
             if n >= TANH_LAG and blocks[n - TANH_LAG][1] == GATE_G:
                 for b in range(ROW_TILES):
                     earlier = blocks[n - TANH_LAG][0]

@@ -27,7 +27,8 @@ HALVES = HIDDEN // BLOCK_ROWS
 CHUNKS = 4 * HALVES
 
 GATE_I, GATE_F, GATE_G, GATE_O = 0, 1, 2, 3
-WH_SCALAR_TILES = 3
+WH_SCALAR_TILES = 4
+SUM_GPSIMD_TILES = 1
 TANH_LAG = 2
 
 FLOPS = 2 * BATCH * 4 * HIDDEN * 2 * K
@@ -226,6 +227,17 @@ def tile_lstmcell_e_kernel(tc, x, h, c, Wx_words, Wx_scales, Wh, bx, bh, out_0, 
             nc.scalar.activation(out=value[:], in_=value[:], func=(TANH if gate == GATE_G else SIGMOID))
             gates[(gate, half, b)] = value
 
+        def finish_c(engine, half, tiles):
+            for b in tiles:
+                i = gates[(GATE_I, half, b)]
+                engine.tensor_mul(out=i[:], in0=i[:], in1=gates[(GATE_G, half, b)][:])
+            for b in tiles:
+                f = gates[(GATE_F, half, b)]
+                engine.tensor_add(out=f[:], in0=f[:], in1=gates[(GATE_I, half, b)][:])
+                nc.sync.dma_start(
+                    out=out_1[b * P : (b + 1) * P, half * BLOCK_ROWS : (half + 1) * BLOCK_ROWS], in_=f[:]
+                )
+
         x_mx = operand("x")
         h_mx = operand("h")
         stationary(x_raw, x_mx, ())
@@ -241,27 +253,28 @@ def tile_lstmcell_e_kernel(tc, x, h, c, Wx_words, Wx_scales, Wh, bx, bh, out_0, 
             cols = slice(half * BLOCK_ROWS, (half + 1) * BLOCK_ROWS)
             if n > 0:
                 x_passes(n)
+            if n > 0 and blocks[n - 1][1] == GATE_G:
+                finish_c(nc.vector, blocks[n - 1][0], range(SUM_GPSIMD_TILES, ROW_TILES))
             if n + 1 < len(blocks):
                 transpose_block(n + 1, range(WH_SCALAR_TILES))
             if n >= TANH_LAG and blocks[n - TANH_LAG][1] == GATE_G:
+                earlier = blocks[n - TANH_LAG][0]
                 for b in range(ROW_TILES):
-                    earlier = blocks[n - TANH_LAG][0]
                     nc.scalar.activation(
                         out=gates[(GATE_G, earlier, b)][:], in_=gates[(GATE_F, earlier, b)][:], func=TANH
                     )
             for b in range(ROW_TILES):
                 h_passes(n, b)
-                f, i, g = [gates.get((e, half, b)) for e in (GATE_F, GATE_I, GATE_G)]
                 if gate == GATE_F:
+                    f = gates[(GATE_F, half, b)]
                     nc.gpsimd.tensor_mul(out=f[:], in0=f[:], in1=c_sb[:, b, cols])
-                if gate == GATE_G:
-                    nc.gpsimd.tensor_mul(out=i[:], in0=i[:], in1=g[:])
-                    nc.gpsimd.tensor_add(out=f[:], in0=f[:], in1=i[:])
-                    nc.sync.dma_start(out=out_1[b * P : (b + 1) * P, cols], in_=f[:])
+                if gate == GATE_G and b < SUM_GPSIMD_TILES:
+                    finish_c(nc.gpsimd, half, (b,))
             if n + 1 < len(blocks):
                 quantise_block(n + 1)
             if gate == GATE_O:
                 for b in range(ROW_TILES):
                     hs = gates[(GATE_O, half, b)]
-                    nc.vector.tensor_mul(out=hs[:], in0=hs[:], in1=gates[(GATE_G, half, b)][:])
+                    multiply = nc.vector.tensor_mul if n + 1 == len(blocks) else nc.gpsimd.tensor_mul
+                    multiply(out=hs[:], in0=hs[:], in1=gates[(GATE_G, half, b)][:])
                     nc.sync.dma_start(out=out_0[b * P : (b + 1) * P, cols], in_=hs[:])

@@ -27,6 +27,7 @@ HALVES = HIDDEN // BLOCK_ROWS
 CHUNKS = 4 * HALVES
 
 GATE_I, GATE_F, GATE_G, GATE_O = 0, 1, 2, 3
+SORTED_BLOCKS = (2, 3, 5)
 WH_SCALAR_TILES = 4
 SUM_GPSIMD_TILES = 1
 TANH_LAG = 2
@@ -41,7 +42,8 @@ def tile_lstmcell_e_kernel(tc, x, h, c, Wx_words, Wx_scales, Wh, bx, bh, out_0, 
 
     with ExitStack() as ctx:
         keep = ctx.enter_context(tc.tile_pool(name="keep", bufs=1))
-        raw_pool = ctx.enter_context(tc.tile_pool(name="raw", bufs=len(blocks) + 2))
+        raw_pool = ctx.enter_context(tc.tile_pool(name="raw", bufs=len(blocks)))
+        sorted_pool = ctx.enter_context(tc.tile_pool(name="sorted", bufs=2))
         grouped_pool = ctx.enter_context(tc.tile_pool(name="grouped", bufs=2))
         wh_mx_pool = ctx.enter_context(tc.tile_pool(name="wh_mx", bufs=2))
         gate_pool = ctx.enter_context(tc.tile_pool(name="gates", bufs=HALVES * ROW_TILES))
@@ -127,21 +129,31 @@ def tile_lstmcell_e_kernel(tc, x, h, c, Wx_words, Wx_scales, Wh, bx, bh, out_0, 
 
         bias_sb = keep.tile([P, CHUNKS, BLOCK_ROWS], F32)
 
-        def spread_bias(q):
-            spread = sum_psum.tile([P, BLOCK_ROWS], F32, name="spread", tag="sum")
-            nc.tensor.matmul(
-                spread[:], lhsT=pick[:, q : q + 1].to_broadcast([P, P]), rhs=bias_rows[:], start=True, stop=True
-            )
-            nc.scalar.copy(out=bias_sb[:, q, :], in_=spread[:])
+        def spread_bias(*chunks):
+            for q in chunks:
+                spread = flip_psum.tile([P, BLOCK_ROWS], F32, name="spread", tag="bank")
+                nc.tensor.matmul(
+                    spread[:], lhsT=pick[:, q : q + 1].to_broadcast([P, P]), rhs=bias_rows[:], start=True, stop=True
+                )
+                nc.scalar.copy(out=bias_sb[:, q, :], in_=spread[:])
 
-        def transpose_tile(raw, r, out, copy_out):
-            words = raw[:, r, :].bitcast(F32)
+        def sort_words(copy, raw, words, first, last):
+            copy(
+                out=words[:, first:last, :, :, :].rearrange("q r s u p -> q (r s) u p"),
+                in_=raw[:, first:last, :].bitcast(F32).rearrange("q r (s p u) -> q (r s) u p", s=PASSES, u=2),
+            )
+
+        def loaded(raw):
+            return lambda r, s, u: raw[:, r, :].bitcast(F32)[:, s * PASS_WORDS + u : (s + 1) * PASS_WORDS : 2]
+
+        def sorted_words(words):
+            return lambda r, s, u: words[:, r, s, u, :]
+
+        def transpose_tile(words_of, r, out, copy_out):
             flipped = flip_psum.tile([P, PASSES, 2, P], F32, tag="bank")
             for s in range(PASSES):
                 for u in range(2):
-                    nc.tensor.transpose(
-                        flipped[:, s, u, :], words[:, s * PASS_WORDS + u : (s + 1) * PASS_WORDS : 2], identity[:]
-                    )
+                    nc.tensor.transpose(flipped[:, s, u, :], words_of(r, s, u), identity[:])
             copy_out(out=out.bitcast(F32), in_=flipped[:].rearrange("p s u n -> p s n u"))
 
         def quantise(grouped, codes, planes):
@@ -159,26 +171,34 @@ def tile_lstmcell_e_kernel(tc, x, h, c, Wx_words, Wx_scales, Wh, bx, bh, out_0, 
                 mx[1][:, r, :, :].rearrange("p s n -> p (s n)"),
             )
 
-        def stationary(raw, mx, scalar_tiles):
+        def stationary(words_of, mx, scalar_tiles, chunks):
             grouped = grouped_pool.tile([P, ROW_TILES, PASSES, P, PACK], BF16, name="kept_grouped", tag="grouped", align_bytes=64)
             for r in range(ROW_TILES):
                 transpose_tile(
-                    raw, r, grouped[:, r, :, :, :], nc.scalar.copy if r in scalar_tiles else nc.vector.tensor_copy
+                    words_of, r, grouped[:, r, :, :, :], nc.scalar.copy if r in scalar_tiles else nc.vector.tensor_copy
                 )
+                spread_bias(*chunks[r : r + 1])
                 if r > 0:
                     quantise_tile(grouped, mx, r - 1)
             quantise_tile(grouped, mx, ROW_TILES - 1)
 
+        wh_sorted = {}
         wh_grouped = {}
         wh_mx = {}
         gates = {}
         sums = {}
 
+        def sort_block(n):
+            words = sorted_pool.tile([P, ROW_TILES, PASSES, 2, P], F32, name="wh_sorted", tag="sorted")
+            sort_words(nc.vector.tensor_copy, wh_raw[n], words, 0, ROW_TILES // 2)
+            sort_words(nc.scalar.copy, wh_raw[n], words, ROW_TILES // 2, ROW_TILES)
+            wh_sorted[n] = words
+
         def transpose_block(n, scalar_tiles):
             wh_grouped[n] = grouped_pool.tile([P, PASSES, BLOCK_ROWS, PACK], BF16, name="wh_grouped", tag="grouped", align_bytes=64)
             for r in range(ROW_TILES):
                 transpose_tile(
-                    wh_raw[n],
+                    sorted_words(wh_sorted[n]) if n in wh_sorted else loaded(wh_raw[n]),
                     r,
                     wh_grouped[n][:, :, r * P : (r + 1) * P, :],
                     nc.scalar.copy if r in scalar_tiles else nc.vector.tensor_copy,
@@ -240,12 +260,15 @@ def tile_lstmcell_e_kernel(tc, x, h, c, Wx_words, Wx_scales, Wh, bx, bh, out_0, 
 
         x_mx = operand("x")
         h_mx = operand("h")
-        stationary(x_raw, x_mx, ())
-        for q in range(CHUNKS):
-            spread_bias(q)
+        stationary(loaded(x_raw), x_mx, (), (0, 1, 2, 3))
         x_passes(0)
-        stationary(h_raw, h_mx, (0, 2))
+        h_sorted = sorted_pool.tile([P, ROW_TILES, PASSES, 2, P], F32, name="h_sorted", tag="sorted")
+        for r in range(0, ROW_TILES, 2):
+            sort_words(nc.vector.tensor_copy, h_raw, h_sorted, r, r + 2)
+        stationary(sorted_words(h_sorted), h_mx, (0, 2), ())
+        spread_bias(4, 5)
         transpose_block(0, (0, 2))
+        spread_bias(6, 7)
         quantise_block(0)
 
         for n in range(len(blocks)):
@@ -270,6 +293,8 @@ def tile_lstmcell_e_kernel(tc, x, h, c, Wx_words, Wx_scales, Wh, bx, bh, out_0, 
                     nc.gpsimd.tensor_mul(out=f[:], in0=f[:], in1=c_sb[:, b, cols])
                 if gate == GATE_G and b < SUM_GPSIMD_TILES:
                     finish_c(nc.gpsimd, half, (b,))
+            if n + 2 in SORTED_BLOCKS:
+                sort_block(n + 2)
             if n + 1 < len(blocks):
                 quantise_block(n + 1)
             if gate == GATE_O:

from contextlib import ExitStack

import concourse.mybir as mybir
from concourse.masks import make_identity

F32 = mybir.dt.float32
BF16 = mybir.dt.bfloat16
I32 = mybir.dt.int32
U32 = mybir.dt.uint32
U8 = mybir.dt.uint8
FP8X4 = mybir.dt.float8_e4m3fn_x4
FP4X4 = mybir.dt.float4_e2m1fn_x4
SIGMOID = mybir.ActivationFunctionType.Sigmoid
TANH = mybir.ActivationFunctionType.Tanh

P = 128
PACK = 4
K_PASS = P * PACK
BATCH = 512
K = 1024
HIDDEN = 1024
PASSES = K // K_PASS
BLOCK_ROWS = 512
ROW_TILES = BLOCK_ROWS // P
PASS_WORDS = K_PASS // 2
HALVES = HIDDEN // BLOCK_ROWS
CHUNKS = 4 * HALVES

GATE_I, GATE_F, GATE_G, GATE_O = 0, 1, 2, 3
SORTED_BLOCKS = (2, 3, 5)
WH_SCALAR_TILES = 4
SUM_GPSIMD_TILES = 1
TANH_LAG = 2

FLOPS = 2 * BATCH * 4 * HIDDEN * 2 * K


def tile_lstmcell_e_kernel(tc, x, h, c, Wx_words, Wx_scales, Wh, bx, bh, out_0, out_1):
    nc = tc.nc
    blocks = [(half, gate) for half in range(HALVES) for gate in (GATE_F, GATE_I, GATE_G)]
    blocks += [(half, GATE_O) for half in range(HALVES)]

    with ExitStack() as ctx:
        keep = ctx.enter_context(tc.tile_pool(name="keep", bufs=1))
        raw_pool = ctx.enter_context(tc.tile_pool(name="raw", bufs=len(blocks)))
        sorted_pool = ctx.enter_context(tc.tile_pool(name="sorted", bufs=2))
        grouped_pool = ctx.enter_context(tc.tile_pool(name="grouped", bufs=2))
        wh_mx_pool = ctx.enter_context(tc.tile_pool(name="wh_mx", bufs=2))
        gate_pool = ctx.enter_context(tc.tile_pool(name="gates", bufs=HALVES * ROW_TILES))
        flip_psum = ctx.enter_context(tc.psum_pool(name="flip", bufs=ROW_TILES))
        sum_psum = ctx.enter_context(tc.psum_pool(name="sums", bufs=ROW_TILES))
        ctx.enter_context(tc.manual_schedule())

        bias_rows = keep.tile([P, BLOCK_ROWS], BF16)
        nc.vector.memset(bias_rows[:].bitcast(I32), 0)
        warm = keep.tile([P, 1], F32)
        nc.vector.memset(warm[:], 0.0)
        wx_planes = {}
        for gate in (GATE_F, GATE_I, GATE_G, GATE_O):
            wx_planes[gate] = keep.tile([P, PASSES, HIDDEN], U8, name="wx_planes%d" % gate, align_bytes=64)
            nc.vector.memset(wx_planes[gate][:].rearrange("p s n -> p (s n)").bitcast(I32), 0)
        identity = keep.tile([P, P], F32)
        make_identity(nc, identity[:])
        pick = keep.tile([P, CHUNKS], BF16)
        nc.gpsimd.tensor_add(out=pick[:], in0=identity[:, 0:CHUNKS], in1=identity[:, CHUNKS : 2 * CHUNKS])

        nc.scalar.dma_start(out=bias_rows[0:CHUNKS, :], in_=bx.rearrange("g (a n) -> (g a) n", n=BLOCK_ROWS))
        nc.scalar.dma_start(
            out=bias_rows[CHUNKS : 2 * CHUNKS, :], in_=bh.rearrange("g (a n) -> (g a) n", n=BLOCK_ROWS)
        )
        nc.scalar.activation(out=warm[:], in_=warm[:], func=SIGMOID)

        def load_rows(rows, pieces):
            raw = raw_pool.tile([P, ROW_TILES, K], BF16)
            step = ROW_TILES // pieces
            for a in range(0, ROW_TILES, step):
                nc.sync.dma_start(
                    out=raw[:, a : a + step, :],
                    in_=rows[a * P : (a + step) * P, :].rearrange("(r p) k -> p r k", p=P),
                )
            return raw

        wx_words = {}
        words_dram = Wx_words.bitcast(I32)
        scales_dram = Wx_scales.bitcast(I32).rearrange("s (q r) n -> r q s n", r=4)

        def load_scales(gate):
            for r in range(4):
                nc.sync.dma_start(
                    out=wx_planes[gate][r:P:32, :, :].bitcast(I32),
                    in_=scales_dram[r, :, gate * PASSES : (gate + 1) * PASSES, :],
                )

        def load_words(gate, half):
            words = keep.tile(
                [P, PASSES, 2 * BLOCK_ROWS], U8, name="wx_words%d_%d" % (gate, half), align_bytes=64
            )
            first = half * BLOCK_ROWS // 2
            nc.sync.dma_start(
                out=words[:].bitcast(I32),
                in_=words_dram[gate * PASSES : (gate + 1) * PASSES, :, first : first + BLOCK_ROWS // 2].rearrange(
                    "s p n -> p s n"
                ),
            )
            wx_words[(gate, half)] = words

        def load_wh(n):
            half, gate = blocks[n]
            return load_rows(Wh[gate, half * BLOCK_ROWS : (half + 1) * BLOCK_ROWS, :], 1)

        c_sb = keep.tile([P, ROW_TILES, HIDDEN], BF16)
        wh_raw = {}
        x_raw = load_rows(x, 4)
        load_scales(GATE_F)
        load_words(GATE_F, 0)
        h_raw = load_rows(h, 2)
        wh_raw[0] = load_wh(0)
        wh_raw[1] = load_wh(1)
        for gate in (GATE_I, GATE_G, GATE_O):
            load_scales(gate)
        load_words(GATE_I, 0)
        wh_raw[2] = load_wh(2)
        load_words(GATE_G, 0)
        nc.sync.dma_start(out=c_sb[:], in_=c.rearrange("(b p) n -> p b n", p=P))
        for n in range(3, len(blocks)):
            half, gate = blocks[n]
            load_words(gate, half)
            wh_raw[n] = load_wh(n)

        bias_sb = keep.tile([P, CHUNKS, BLOCK_ROWS], F32)

        def spread_bias(*chunks):
            for q in chunks:
                spread = flip_psum.tile([P, BLOCK_ROWS], F32, name="spread", tag="bank")
                nc.tensor.matmul(
                    spread[:], lhsT=pick[:, q : q + 1].to_broadcast([P, P]), rhs=bias_rows[:], start=True, stop=True
                )
                nc.scalar.copy(out=bias_sb[:, q, :], in_=spread[:])

        def sort_words(copy, raw, words, first, last):
            copy(
                out=words[:, first:last, :, :, :].rearrange("q r s u p -> q (r s) u p"),
                in_=raw[:, first:last, :].bitcast(F32).rearrange("q r (s p u) -> q (r s) u p", s=PASSES, u=2),
            )

        def loaded(raw):
            return lambda r, s, u: raw[:, r, :].bitcast(F32)[:, s * PASS_WORDS + u : (s + 1) * PASS_WORDS : 2]

        def sorted_words(words):
            return lambda r, s, u: words[:, r, s, u, :]

        def transpose_tile(words_of, r, out, copy_out):
            flipped = flip_psum.tile([P, PASSES, 2, P], F32, tag="bank")
            for s in range(PASSES):
                for u in range(2):
                    nc.tensor.transpose(flipped[:, s, u, :], words_of(r, s, u), identity[:])
            copy_out(out=out.bitcast(F32), in_=flipped[:].rearrange("p s u n -> p s n u"))

        def quantise(grouped, codes, planes):
            nc.vector.quantize_mx(out=codes.bitcast(FP8X4), scales=planes, in_=grouped)

        def operand(name):
            codes = keep.tile([P, ROW_TILES, PASSES, P], U32, name=name + "_codes", align_bytes=64)
            planes = keep.tile([P, ROW_TILES, PASSES, P], U8, name=name + "_planes", align_bytes=64)
            return codes, planes

        def quantise_tile(grouped, mx, r):
            quantise(
                grouped[:, r, :, :, :].rearrange("p s n t -> p (s n t)"),
                mx[0][:, r, :, :].rearrange("p s n -> p (s n)"),
                mx[1][:, r, :, :].rearrange("p s n -> p (s n)"),
            )

        def stationary(words_of, mx, scalar_tiles, chunks):
            grouped = grouped_pool.tile([P, ROW_TILES, PASSES, P, PACK], BF16, name="kept_grouped", tag="grouped", align_bytes=64)
            for r in range(ROW_TILES):
                transpose_tile(
                    words_of, r, grouped[:, r, :, :, :], nc.scalar.copy if r in scalar_tiles else nc.vector.tensor_copy
                )
                spread_bias(*chunks[r : r + 1])
                if r > 0:
                    quantise_tile(grouped, mx, r - 1)
            quantise_tile(grouped, mx, ROW_TILES - 1)

        wh_sorted = {}
        wh_grouped = {}
        wh_mx = {}
        gates = {}
        sums = {}

        def sort_block(n):
            words = sorted_pool.tile([P, ROW_TILES, PASSES, 2, P], F32, name="wh_sorted", tag="sorted")
            sort_words(nc.vector.tensor_copy, wh_raw[n], words, 0, ROW_TILES // 2)
            sort_words(nc.scalar.copy, wh_raw[n], words, ROW_TILES // 2, ROW_TILES)
            wh_sorted[n] = words

        def transpose_block(n, scalar_tiles):
            wh_grouped[n] = grouped_pool.tile([P, PASSES, BLOCK_ROWS, PACK], BF16, name="wh_grouped", tag="grouped", align_bytes=64)
            for r in range(ROW_TILES):
                transpose_tile(
                    sorted_words(wh_sorted[n]) if n in wh_sorted else loaded(wh_raw[n]),
                    r,
                    wh_grouped[n][:, :, r * P : (r + 1) * P, :],
                    nc.scalar.copy if r in scalar_tiles else nc.vector.tensor_copy,
                )

        def quantise_block(n):
            codes = wh_mx_pool.tile([P, PASSES, BLOCK_ROWS], U32, name="wh_codes", align_bytes=64)
            planes = wh_mx_pool.tile([P, PASSES, BLOCK_ROWS], U8, name="wh_planes", align_bytes=64)
            quantise(
                wh_grouped[n][:].rearrange("p s n t -> p (s n t)"),
                codes[:].rearrange("p s n -> p (s n)"),
                planes[:].rearrange("p s n -> p (s n)"),
            )
            wh_mx[n] = (codes, planes)

        def x_passes(n):
            half, gate = blocks[n]
            for b in range(ROW_TILES):
                sums[b] = sum_psum.tile([P, BLOCK_ROWS], F32, name="acc", tag="sum")
                for s in range(PASSES):
                    nc.tensor.matmul_mx(
                        out=sums[b][:],
                        lhsT=x_mx[0][:, b, s, :].bitcast(FP8X4),
                        lhsT_scale=x_mx[1][:, b, s, :],
                        rhs=wx_words[(gate, half)][:, s, :].bitcast(FP4X4),
                        rhs_scale=wx_planes[gate][:, s, half * BLOCK_ROWS : (half + 1) * BLOCK_ROWS],
                        start=(s == 0),
                        stop=False,
                    )

        def h_passes(n, b):
            half, gate = blocks[n]
            wh_codes, wh_planes = wh_mx[n]
            for s in range(PASSES):
                nc.tensor.matmul_mx(
                    out=sums[b][:],
                    lhsT=h_mx[0][:, b, s, :].bitcast(FP8X4),
                    lhsT_scale=h_mx[1][:, b, s, :],
                    rhs=wh_codes[:, s, :].bitcast(FP8X4),
                    rhs_scale=wh_planes[:, s, :],
                    start=False,
                    stop=(s == PASSES - 1),
                )
            value = gate_pool.tile([P, BLOCK_ROWS], F32, name="gate%d" % gate, tag="gate%d" % gate)
            nc.vector.tensor_add(out=value[:], in0=sums[b][:], in1=bias_sb[:, gate * HALVES + half, :])
            nc.scalar.activation(out=value[:], in_=value[:], func=(TANH if gate == GATE_G else SIGMOID))
            gates[(gate, half, b)] = value

        def finish_c(engine, half, tiles):
            for b in tiles:
                i = gates[(GATE_I, half, b)]
                engine.tensor_mul(out=i[:], in0=i[:], in1=gates[(GATE_G, half, b)][:])
            for b in tiles:
                f = gates[(GATE_F, half, b)]
                engine.tensor_add(out=f[:], in0=f[:], in1=gates[(GATE_I, half, b)][:])
                nc.sync.dma_start(
                    out=out_1[b * P : (b + 1) * P, half * BLOCK_ROWS : (half + 1) * BLOCK_ROWS], in_=f[:]
                )

        x_mx = operand("x")
        h_mx = operand("h")
        stationary(loaded(x_raw), x_mx, (), (0, 1, 2, 3))
        x_passes(0)
        h_sorted = sorted_pool.tile([P, ROW_TILES, PASSES, 2, P], F32, name="h_sorted", tag="sorted")
        for r in range(0, ROW_TILES, 2):
            sort_words(nc.vector.tensor_copy, h_raw, h_sorted, r, r + 2)
        stationary(sorted_words(h_sorted), h_mx, (0, 2), ())
        spread_bias(4, 5)
        transpose_block(0, (0, 2))
        spread_bias(6, 7)
        quantise_block(0)

        for n in range(len(blocks)):
            half, gate = blocks[n]
            cols = slice(half * BLOCK_ROWS, (half + 1) * BLOCK_ROWS)
            if n > 0:
                x_passes(n)
            if n > 0 and blocks[n - 1][1] == GATE_G:
                finish_c(nc.vector, blocks[n - 1][0], range(SUM_GPSIMD_TILES, ROW_TILES))
            if n + 1 < len(blocks):
                transpose_block(n + 1, range(WH_SCALAR_TILES))
            if n >= TANH_LAG and blocks[n - TANH_LAG][1] == GATE_G:
                earlier = blocks[n - TANH_LAG][0]
                for b in range(ROW_TILES):
                    nc.scalar.activation(
                        out=gates[(GATE_G, earlier, b)][:], in_=gates[(GATE_F, earlier, b)][:], func=TANH
                    )
            for b in range(ROW_TILES):
                h_passes(n, b)
                if gate == GATE_F:
                    f = gates[(GATE_F, half, b)]
                    nc.gpsimd.tensor_mul(out=f[:], in0=f[:], in1=c_sb[:, b, cols])
                if gate == GATE_G and b < SUM_GPSIMD_TILES:
                    finish_c(nc.gpsimd, half, (b,))
            if n + 2 in SORTED_BLOCKS:
                sort_block(n + 2)
            if n + 1 < len(blocks):
                quantise_block(n + 1)
            if gate == GATE_O:
                for b in range(ROW_TILES):
                    hs = gates[(GATE_O, half, b)]
                    multiply = nc.vector.tensor_mul if n + 1 == len(blocks) else nc.gpsimd.tensor_mul
                    multiply(out=hs[:], in0=hs[:], in1=gates[(GATE_G, half, b)][:])
                    nc.sync.dma_start(out=out_0[b * P : (b + 1) * P, cols], in_=hs[:])
